import numpy as np
import ml_dtypes


def mxq(x, axis, fmt="e4m3"):
    dtype, down = {"e4m3": (ml_dtypes.float8_e4m3fn, 7), "e5m2": (ml_dtypes.float8_e5m2, 14)}[fmt]
    v = np.moveaxis(np.asarray(x, np.float32).astype(ml_dtypes.bfloat16).astype(np.float64), axis, -1)
    blocks = v.reshape(v.shape[:-1] + (-1, 32))
    amax = np.abs(blocks).max(-1, keepdims=True)
    byte = np.maximum(np.where(amax > 0, np.frexp(amax)[1] - 1 + 127, 0) - down, 1)
    scale = np.exp2(byte - 127.0)
    codes = (blocks / scale).astype(np.float32).astype(dtype).astype(np.float64)
    return np.moveaxis((codes * scale).reshape(v.shape), -1, axis)


WIDE = False


def mx_kscale(k):
    if not WIDE:
        return np.ones(k)
    levels = np.array([10, -10, 5, -5, 0])
    a = np.random.permutation(np.resize(levels, k // 512 * 4)).reshape(k // 512, 4)
    idx = np.arange(k)
    return np.exp2(a[idx // 512, idx % 128 // 32])


BF16 = ml_dtypes.bfloat16


def bf(x):
    return np.asarray(x, np.float32).astype(BF16)


def f64(x):
    return np.asarray(x).astype(np.float64)


N, DB, DV, DL, DC, T, DO = 8192, 500, 500, 256, 128, 12, 256
KB, KV = DB + T, DV + T
LN_EPS = 1e-5
ERF_TERMS = 100


def erf(v):
    a = np.clip(v, -6.0, 6.0)
    term = a.copy()
    tot = a.copy()
    for n in range(1, ERF_TERMS):
        term = term * (2.0 * a * a) / (2.0 * n + 1.0)
        tot = tot + term
    return 2.0 / np.sqrt(np.pi) * np.exp(-a * a) * tot


def gelu_erf(v):
    return 0.5 * v * (1.0 + erf(v / np.sqrt(2.0)))


def t2v(t, w0, w, b):
    v0 = w0 * t + b[0]
    v = np.sin(w * t[:, None] + b[1:])
    return np.concatenate([v0[:, None], v], axis=-1)


def branch(z, gamma, beta, W):
    mu = z.mean(-1, keepdims=True)
    var = np.square(z - mu).mean(-1, keepdims=True)
    zn = (z - mu) / np.sqrt(var + LN_EPS) * gamma + beta
    return gelu_erf(mxq(zn, 1, "e4m3") @ mxq(W, 0, "e4m3"))


def rows(d):
    return np.random.standard_normal((N, d)) * (0.5 + np.random.uniform(size=(N, 1))) + 0.3 * np.random.standard_normal((N, 1))


def setup_inputs():
    sb, sv = mx_kscale(KB), mx_kscale(KV)
    return {"x_bill": bf(rows(DB)), "ts_bill": bf(np.random.uniform(size=N)),
            "x_bill_version": bf(rows(DV)), "ts_bill_version": bf(np.random.uniform(size=N)),
            "w0": bf(3.0 + 0.5 * np.random.standard_normal(1)),
            "w": bf(3.0 * np.random.standard_normal(T - 1)),
            "b": bf(1.5 + 0.5 * np.random.standard_normal(T)),
            "gamma_bill": bf((1.0 + 0.1 * np.random.standard_normal(KB)) * sb),
            "beta_bill": bf(0.1 * np.random.standard_normal(KB) * sb),
            "W_bill": bf(np.random.standard_normal((KB, DO)) * np.sqrt(2.0 / KB) / sb[:, None]),
            "gamma_bill_version": bf((1.0 + 0.1 * np.random.standard_normal(KV)) * sv),
            "beta_bill_version": bf(0.1 * np.random.standard_normal(KV) * sv),
            "W_bill_version": bf(np.random.standard_normal((KV, DO)) * np.sqrt(2.0 / KV) / sv[:, None])}


def reference(x_bill, ts_bill, x_bill_version, ts_bill_version, w0, w, b,
              gamma_bill, beta_bill, W_bill, gamma_bill_version, beta_bill_version, W_bill_version):
    w0, w, b = f64(w0), f64(w), f64(b)
    zb = np.concatenate([f64(x_bill), t2v(f64(ts_bill), w0, w, b)], axis=1)
    zv = np.concatenate([f64(x_bill_version), t2v(f64(ts_bill_version), w0, w, b)], axis=1)
    out_bill = branch(zb, f64(gamma_bill), f64(beta_bill), f64(W_bill))
    out_bv = branch(zv, f64(gamma_bill_version), f64(beta_bill_version), f64(W_bill_version))
    return np.stack([out_bill, out_bv], axis=0)

@@ -1,0 +1,315 @@
+import math
+from contextlib import ExitStack
+
+import concourse.mybir as mybir
+from concourse.masks import make_identity
+
+F32 = mybir.dt.float32
+BF16 = mybir.dt.bfloat16
+U32 = mybir.dt.uint32
+U8 = mybir.dt.uint8
+FP8X4 = mybir.dt.float8_e4m3fn_x4
+ALU = mybir.AluOpType
+ACT = mybir.ActivationFunctionType
+
+P = 128
+ROWS = 8192
+RAW = 500
+T2V = 12
+K = RAW + T2V
+PACK = 4
+D_OUT = 256
+KINDS = 2
+TILES = ROWS // P
+GROUP = 4
+GROUPS = TILES // GROUP
+LN_EPS = 1e-5
+ROUND_MAGIC = 12582912.0
+BODY = 496
+TAIL = K - BODY
+SCALAR_SHARE = 2
+LOAD_AHEAD = 6
+STATS_AHEAD = 4
+NORM_AHEAD = 2
+
+FLOPS = 2 * KINDS * ROWS * K * D_OUT
+
+
+def tile_featureprojector_pa_t_kernel(
+    tc,
+    x_bill,
+    ts_bill,
+    x_bill_version,
+    ts_bill_version,
+    w0,
+    w,
+    b,
+    gamma_bill,
+    beta_bill,
+    W_bill,
+    gamma_bill_version,
+    beta_bill_version,
+    W_bill_version,
+    out,
+):
+    nc = tc.nc
+    xs = [x_bill, x_bill_version]
+    stamps = [ts_bill, ts_bill_version]
+    weights = [W_bill, W_bill_version]
+    column_vectors = [gamma_bill, beta_bill, gamma_bill_version, beta_bill_version]
+
+    with ExitStack() as ctx:
+        keep = ctx.enter_context(tc.tile_pool(name="keep", bufs=1))
+        x_pool = ctx.enter_context(tc.tile_pool(name="x_pool", bufs=LOAD_AHEAD - NORM_AHEAD + 2))
+        small = ctx.enter_context(tc.tile_pool(name="small", bufs=STATS_AHEAD - NORM_AHEAD + 2))
+        u_pool = ctx.enter_context(tc.tile_pool(name="u_pool", bufs=NORM_AHEAD + 2))
+        q_pool = ctx.enter_context(tc.tile_pool(name="q_pool", bufs=3))
+        o_pool = ctx.enter_context(tc.tile_pool(name="o_pool", bufs=3))
+        psum_t = ctx.enter_context(tc.psum_pool(name="psum_t", bufs=6))
+        psum_o = ctx.enter_context(tc.psum_pool(name="psum_o", bufs=2))
+
+        ts_bf = keep.tile([P, KINDS, TILES], BF16, name="ts_bf")
+        for kind in range(KINDS):
+            nc.sync.dma_start(out=ts_bf[:, kind, :], in_=stamps[kind].rearrange("(p t) -> p t", t=TILES))
+        w0_bf = keep.tile([P, 1], BF16, name="w0_bf")
+        w_bf = keep.tile([P, T2V - 1], BF16, name="w_bf")
+        b_bf = keep.tile([P, T2V], BF16, name="b_bf")
+        nc.sync.dma_start(out=w0_bf[:], in_=w0.partition_broadcast(P))
+        nc.sync.dma_start(out=w_bf[:], in_=w.partition_broadcast(P))
+        nc.sync.dma_start(out=b_bf[:], in_=b.partition_broadcast(P))
+
+        def load_group(g):
+            kind, first = divmod(g, GROUPS)
+            first *= GROUP
+            x_sb = x_pool.tile([P, GROUP, RAW], BF16, name="x_sb")
+            rows = xs[kind].rearrange("(p t) k -> p t k", t=TILES)
+            nc.sync.dma_start(out=x_sb[:], in_=rows[:, first : first + GROUP, :])
+            return x_sb
+
+        x_tiles = {0: load_group(0)}
+
+        vec_bf = keep.tile([P, P], BF16, name="vec_bf")
+        nc.vector.memset(vec_bf[:], 0.0)
+        for v in range(len(column_vectors)):
+            nc.sync.dma_start(
+                out=vec_bf[PACK * v : PACK * (v + 1), :],
+                in_=column_vectors[v].rearrange("(j c) -> j c", c=P),
+            )
+        w_raw = []
+        for kind in range(KINDS):
+            raw = keep.tile([P, PACK, D_OUT], BF16, name="w_raw%d" % kind)
+            nc.sync.dma_start(out=raw[:], in_=weights[kind].rearrange("(t p) n -> p t n", p=P))
+            w_raw.append(raw)
+        for g in range(1, LOAD_AHEAD - STATS_AHEAD):
+            x_tiles[g] = load_group(g)
+
+        identity = keep.tile([P, P], F32, name="identity")
+        make_identity(nc, identity[:])
+        neg_half = keep.tile([P, GROUP, 1], F32, name="neg_half")
+        nc.gpsimd.memset(neg_half[:], -0.5)
+
+        slope = keep.tile([P, T2V], F32, name="slope")
+        phase = keep.tile([P, T2V], F32, name="phase")
+        turn = 1.0 / (2.0 * math.pi)
+        nc.vector.tensor_copy(out=slope[:, 0:1], in_=w0_bf[:])
+        nc.vector.tensor_copy(out=phase[:, 0:1], in_=b_bf[:, 0:1])
+        nc.vector.tensor_scalar(out=slope[:, 1:T2V], in0=w_bf[:], scalar1=turn, scalar2=None, op0=ALU.mult)
+        nc.vector.tensor_scalar(out=phase[:, 1:T2V], in0=b_bf[:, 1:T2V], scalar1=turn, scalar2=None, op0=ALU.mult)
+        all_tiles = KINDS * TILES
+        feat = keep.tile([P, T2V, all_tiles], F32, name="feat")
+        for j in range(T2V):
+            nc.scalar.activation(
+                out=feat[:, j, :],
+                in_=ts_bf[:].rearrange("p a t -> p (a t)"),
+                func=ACT.Identity,
+                scale=slope[:, j : j + 1],
+                bias=phase[:, j : j + 1],
+            )
+        sines = feat[:, 1:T2V, :]
+        whole = keep.tile([P, T2V - 1, all_tiles], F32, name="whole")
+        nc.vector.tensor_scalar(
+            out=whole[:], in0=sines, scalar1=ROUND_MAGIC, scalar2=ROUND_MAGIC, op0=ALU.add, op1=ALU.subtract
+        )
+        nc.vector.tensor_tensor(out=sines, in0=sines, in1=whole[:], op=ALU.subtract)
+        nc.scalar.activation(out=sines, in_=sines, func=ACT.Sin, scale=2.0 * math.pi)
+
+        squares = keep.tile([P, T2V, all_tiles], F32, name="squares")
+        nc.scalar.activation(out=squares[:], in_=feat[:], func=ACT.Square)
+        feat_sum = keep.tile([P, all_tiles], F32, name="feat_sum")
+        feat_sq = keep.tile([P, all_tiles], F32, name="feat_sq")
+        nc.vector.tensor_reduce(
+            out=feat_sum[:], in_=feat[:].rearrange("p j g -> p g j"), axis=mybir.AxisListType.X, op=ALU.add
+        )
+        nc.vector.tensor_reduce(
+            out=feat_sq[:], in_=squares[:].rearrange("p j g -> p g j"), axis=mybir.AxisListType.X, op=ALU.add
+        )
+        stats = keep.tile([P, all_tiles, 9], F32, name="stats")
+        feat_stats = stats[:, :, 6:9]
+        nc.vector.memset(feat_stats[:, :, 0:1], float(T2V))
+        nc.vector.tensor_scalar(
+            out=feat_stats[:, :, 1:2], in0=feat_sum[:].unsqueeze(2), scalar1=1.0 / T2V, scalar2=None, op0=ALU.mult
+        )
+        nc.vector.tensor_tensor(
+            out=feat_stats[:, :, 2:3], in0=feat_sum[:].unsqueeze(2), in1=feat_stats[:, :, 1:2], op=ALU.mult
+        )
+        nc.vector.tensor_tensor(
+            out=feat_stats[:, :, 2:3], in0=feat_sq[:].unsqueeze(2), in1=feat_stats[:, :, 2:3], op=ALU.subtract
+        )
+        nc.vector.tensor_scalar(
+            out=feat_stats[:, :, 2:3], in0=feat_stats[:, :, 2:3], scalar1=K * LN_EPS, scalar2=None, op0=ALU.add
+        )
+
+        vec_f32 = keep.tile([P, P], F32, name="vec_f32")
+        nc.vector.tensor_copy(out=vec_f32[:], in_=vec_bf[:])
+        vec_t = psum_t.tile([P, PACK * P], F32, name="tp")
+        nc.tensor.transpose(vec_t[:, 0:P], vec_f32[:], identity[:])
+        col = keep.tile([P, PACK * len(column_vectors)], F32, name="col")
+        nc.vector.tensor_copy(out=col[:], in_=vec_t[:, 0 : PACK * len(column_vectors)])
+
+        w_codes = []
+        w_scales = []
+        for kind in range(KINDS):
+            grouped_w = keep.tile([P, D_OUT, PACK], BF16, name="grouped_w%d" % kind, align_bytes=64)
+            nc.scalar.copy(
+                out=grouped_w[:].rearrange("p (c i) t -> p c t i", i=4),
+                in_=w_raw[kind][:].rearrange("p t (c i) -> p c t i", i=4),
+            )
+            codes = keep.tile([P, D_OUT], U32, name="w_codes%d" % kind, align_bytes=64)
+            scales = keep.tile([P, D_OUT], U8, name="w_scales%d" % kind, align_bytes=64)
+            nc.vector.quantize_mx(
+                out=codes[:].bitcast(FP8X4), scales=scales[:], in_=grouped_w[:].rearrange("p n t -> p (n t)")
+            )
+            w_codes.append(codes)
+            w_scales.append(scales)
+
+        def statistics(g):
+            x_sb = x_tiles[g]
+            mean_var = small.tile([P, GROUP, 2], F32, name="mean_var")
+            for i in range(GROUP):
+                nc.vector.bn_stats(out=stats[:, g * GROUP + i, 0:6], in_=x_sb[:, i, :])
+            for i in range(GROUP):
+                nc.vector.bn_aggr(out=mean_var[:, i, :], in_=stats[:, g * GROUP + i, :])
+            rstd = small.tile([P, GROUP, 1], F32, name="rstd")
+            nc.gpsimd.tensor_tensor(out=rstd[:], in0=mean_var[:, :, 1:2], in1=neg_half[:], op=ALU.pow)
+            return mean_var, rstd
+
+        def normalise(g):
+            x_sb = x_tiles[g]
+            mean_var, rstd = row_stats[g]
+            shift = small.tile([P, GROUP, 1], F32, name="shift")
+            nc.vector.scalar_tensor_tensor(
+                out=shift[:], in0=mean_var[:, :, 0:1], scalar=-1.0, in1=rstd[:], op0=ALU.mult, op1=ALU.mult
+            )
+            u = u_pool.tile([P, GROUP, K], F32, name="u")
+            for i in range(GROUP):
+                if i < SCALAR_SHARE:
+                    nc.scalar.activation(
+                        out=u[:, i, 0:BODY],
+                        in_=x_sb[:, i, 0:BODY],
+                        func=ACT.Identity,
+                        scale=rstd[:, i, :],
+                        bias=shift[:, i, :],
+                    )
+                else:
+                    nc.gpsimd.tensor_scalar(
+                        out=u[:, i, 0:BODY],
+                        in0=x_sb[:, i, 0:BODY],
+                        scalar1=rstd[:, i, :],
+                        scalar2=shift[:, i, :],
+                        op0=ALU.mult,
+                        op1=ALU.add,
+                    )
+            centred = small.tile([P, GROUP, TAIL], F32, name="centred")
+            nc.gpsimd.tensor_tensor(
+                out=centred[:, :, 0 : RAW - BODY],
+                in0=x_sb[:, :, BODY:RAW],
+                in1=mean_var[:, :, 0:1].to_broadcast([P, GROUP, RAW - BODY]),
+                op=ALU.subtract,
+            )
+            nc.gpsimd.tensor_tensor(
+                out=centred[:, :, RAW - BODY : TAIL],
+                in0=feat[:, :, g * GROUP : (g + 1) * GROUP].rearrange("p j g -> p g j"),
+                in1=mean_var[:, :, 0:1].to_broadcast([P, GROUP, T2V]),
+                op=ALU.subtract,
+            )
+            nc.gpsimd.tensor_tensor(
+                out=u[:, :, BODY:K], in0=centred[:], in1=rstd[:].to_broadcast([P, GROUP, TAIL]), op=ALU.mult
+            )
+            return u
+
+        def transpose_and_scale(g):
+            kind = g // GROUPS
+            u = u_tiles[g]
+            planes = q_pool.tile([P, PACK, GROUP * P], BF16, name="planes")
+            for j in range(PACK):
+                tp = psum_t.tile([P, GROUP * P], F32, name="tp")
+                for i in range(GROUP):
+                    nc.tensor.transpose(tp[:, i * P : (i + 1) * P], u[:, i, j * P : (j + 1) * P], identity[:])
+                nc.scalar.activation(
+                    out=planes[:, j, :],
+                    in_=tp[:],
+                    func=ACT.Identity,
+                    scale=col[:, 8 * kind + j : 8 * kind + j + 1],
+                    bias=col[:, 8 * kind + PACK + j : 8 * kind + PACK + j + 1],
+                )
+            return planes
+
+        def regroup(g):
+            planes = plane_tiles[g]
+            grouped = q_pool.tile([P, GROUP * P, PACK], BF16, name="grouped", align_bytes=64)
+            nc.vector.tensor_copy(
+                out=grouped[:].rearrange("p (c i) t -> p c t i", i=4),
+                in_=planes[:].rearrange("p t (c i) -> p c t i", i=4),
+            )
+            return grouped
+
+        def quantise(g):
+            grouped = grouped_tiles[g]
+            codes = q_pool.tile([P, GROUP * P], U32, name="codes", align_bytes=64)
+            scales = q_pool.tile([P, GROUP * P], U8, name="scales", align_bytes=64)
+            nc.vector.quantize_mx(
+                out=codes[:].bitcast(FP8X4), scales=scales[:], in_=grouped[:].rearrange("p r t -> p (r t)")
+            )
+            return codes, scales
+
+        def project_and_store(g, codes, scales):
+            kind, first = divmod(g, GROUPS)
+            first *= GROUP
+            o_sb = o_pool.tile([P, GROUP, D_OUT], F32, name="o_sb")
+            for pair in range(GROUP // 2):
+                acc = psum_o.tile([P, 2, D_OUT], F32, name="acc")
+                for i in range(2):
+                    rows = slice((2 * pair + i) * P, (2 * pair + i + 1) * P)
+                    nc.tensor.matmul_mx(
+                        out=acc[:, i, :],
+                        lhsT=codes[:, rows].bitcast(FP8X4),
+                        lhsT_scale=scales[:, rows],
+                        rhs=w_codes[kind][:].bitcast(FP8X4),
+                        rhs_scale=w_scales[kind][:],
+                        start=True,
+                        stop=True,
+                    )
+                nc.scalar.activation(out=o_sb[:, 2 * pair : 2 * pair + 2, :], in_=acc[:], func=ACT.Gelu)
+            out_rows = out[kind].rearrange("(p t) d -> p t d", t=TILES)
+            nc.sync.dma_start(out=out_rows[:, first : first + GROUP, :], in_=o_sb[:])
+
+        n_groups = KINDS * GROUPS
+        row_stats = {}
+        u_tiles = {}
+        plane_tiles = {}
+        grouped_tiles = {}
+        with tc.manual_schedule():
+            for n in range(-STATS_AHEAD, n_groups + 1):
+                if 0 <= n - 1:
+                    grouped_tiles[n - 1] = regroup(n - 1)
+                if 0 <= n < n_groups:
+                    plane_tiles[n] = transpose_and_scale(n)
+                if 0 <= n + NORM_AHEAD < n_groups:
+                    u_tiles[n + NORM_AHEAD] = normalise(n + NORM_AHEAD)
+                if 0 <= n - 1:
+                    codes, scales = quantise(n - 1)
+                    project_and_store(n - 1, codes, scales)
+                if LOAD_AHEAD - STATS_AHEAD <= n + LOAD_AHEAD < n_groups:
+                    x_tiles[n + LOAD_AHEAD] = load_group(n + LOAD_AHEAD)
+                if n + STATS_AHEAD < n_groups:
+                    row_stats[n + STATS_AHEAD] = statistics(n + STATS_AHEAD)

@@ -28,9 +28,10 @@ ROUND_MAGIC = 12582912.0
 BODY = 496
 TAIL = K - BODY
 SCALAR_SHARE = 2
-LOAD_AHEAD = 6
-STATS_AHEAD = 4
-NORM_AHEAD = 2
+T_BANKS = 6
+LOAD_AHEAD = 8
+STATS_AHEAD = 6
+NORM_AHEAD = 4
 
 FLOPS = 2 * KINDS * ROWS * K * D_OUT
 
@@ -65,7 +66,7 @@ def tile_featureprojector_pa_t_kernel(
         u_pool = ctx.enter_context(tc.tile_pool(name="u_pool", bufs=NORM_AHEAD + 2))
         q_pool = ctx.enter_context(tc.tile_pool(name="q_pool", bufs=3))
         o_pool = ctx.enter_context(tc.tile_pool(name="o_pool", bufs=3))
-        psum_t = ctx.enter_context(tc.psum_pool(name="psum_t", bufs=6))
+        psum_t = ctx.enter_context(tc.psum_pool(name="psum_t", bufs=T_BANKS))
         psum_o = ctx.enter_context(tc.psum_pool(name="psum_o", bufs=2))
 
         ts_bf = keep.tile([P, KINDS, TILES], BF16, name="ts_bf")
@@ -237,22 +238,25 @@ def tile_featureprojector_pa_t_kernel(
             )
             return u
 
-        def transpose_and_scale(g):
+        def transpose_bank(m):
+            g, j = divmod(m, PACK)
+            tp = psum_t.tile([P, GROUP * P], F32, name="tp")
+            for i in range(GROUP):
+                nc.tensor.transpose(tp[:, i * P : (i + 1) * P], u_tiles[g][:, i, j * P : (j + 1) * P], identity[:])
+            return tp
+
+        def scale_bank(m):
+            g, j = divmod(m, PACK)
             kind = g // GROUPS
-            u = u_tiles[g]
-            planes = q_pool.tile([P, PACK, GROUP * P], BF16, name="planes")
-            for j in range(PACK):
-                tp = psum_t.tile([P, GROUP * P], F32, name="tp")
-                for i in range(GROUP):
-                    nc.tensor.transpose(tp[:, i * P : (i + 1) * P], u[:, i, j * P : (j + 1) * P], identity[:])
-                nc.scalar.activation(
-                    out=planes[:, j, :],
-                    in_=tp[:],
-                    func=ACT.Identity,
-                    scale=col[:, 8 * kind + j : 8 * kind + j + 1],
-                    bias=col[:, 8 * kind + PACK + j : 8 * kind + PACK + j + 1],
-                )
-            return planes
+            if j == 0:
+                plane_tiles[g] = q_pool.tile([P, PACK, GROUP * P], BF16, name="planes")
+            nc.scalar.activation(
+                out=plane_tiles[g][:, j, :],
+                in_=banks[m][:],
+                func=ACT.Identity,
+                scale=col[:, 8 * kind + j : 8 * kind + j + 1],
+                bias=col[:, 8 * kind + PACK + j : 8 * kind + PACK + j + 1],
+            )
 
         def regroup(g):
             planes = plane_tiles[g]
@@ -272,10 +276,10 @@ def tile_featureprojector_pa_t_kernel(
             )
             return codes, scales
 
-        def project_and_store(g, codes, scales):
-            kind, first = divmod(g, GROUPS)
-            first *= GROUP
-            o_sb = o_pool.tile([P, GROUP, D_OUT], F32, name="o_sb")
+        def project(g):
+            kind = g // GROUPS
+            codes, scales = code_tiles[g]
+            accs = []
             for pair in range(GROUP // 2):
                 acc = psum_o.tile([P, 2, D_OUT], F32, name="acc")
                 for i in range(2):
@@ -289,26 +293,43 @@ def tile_featureprojector_pa_t_kernel(
                         start=True,
                         stop=True,
                     )
-                nc.scalar.activation(out=o_sb[:, 2 * pair : 2 * pair + 2, :], in_=acc[:], func=ACT.Gelu)
+                accs.append(acc)
+            return accs
+
+        def gelu_and_store(g):
+            kind, first = divmod(g, GROUPS)
+            first *= GROUP
+            o_sb = o_pool.tile([P, GROUP, D_OUT], F32, name="o_sb")
+            for pair in range(GROUP // 2):
+                nc.scalar.activation(out=o_sb[:, 2 * pair : 2 * pair + 2, :], in_=acc_tiles[g][pair][:], func=ACT.Gelu)
             out_rows = out[kind].rearrange("(p t) d -> p t d", t=TILES)
             nc.sync.dma_start(out=out_rows[:, first : first + GROUP, :], in_=o_sb[:])
 
         n_groups = KINDS * GROUPS
         row_stats = {}
         u_tiles = {}
+        banks = {}
         plane_tiles = {}
         grouped_tiles = {}
+        code_tiles = {}
+        acc_tiles = {}
         with tc.manual_schedule():
-            for n in range(-STATS_AHEAD, n_groups + 1):
-                if 0 <= n - 1:
+            for n in range(-STATS_AHEAD, n_groups + 2):
+                if 0 <= n - 2 < n_groups:
+                    code_tiles[n - 2] = quantise(n - 2)
+                    acc_tiles[n - 2] = project(n - 2)
+                for j in range(PACK):
+                    if 0 <= n < n_groups:
+                        scale_bank(PACK * n + j)
+                    ahead = PACK * n + j + T_BANKS
+                    if 0 <= ahead < PACK * n_groups:
+                        banks[ahead] = transpose_bank(ahead)
+                if 0 <= n - 1 < n_groups:
                     grouped_tiles[n - 1] = regroup(n - 1)
-                if 0 <= n < n_groups:
-                    plane_tiles[n] = transpose_and_scale(n)
+                if 0 <= n - 2 < n_groups:
+                    gelu_and_store(n - 2)
                 if 0 <= n + NORM_AHEAD < n_groups:
                     u_tiles[n + NORM_AHEAD] = normalise(n + NORM_AHEAD)
-                if 0 <= n - 1:
-                    codes, scales = quantise(n - 1)
-                    project_and_store(n - 1, codes, scales)
                 if LOAD_AHEAD - STATS_AHEAD <= n + LOAD_AHEAD < n_groups:
                     x_tiles[n + LOAD_AHEAD] = load_group(n + LOAD_AHEAD)
                 if n + STATS_AHEAD < n_groups:

@@ -27,11 +27,10 @@ LN_EPS = 1e-5
 ROUND_MAGIC = 12582912.0
 BODY = 496
 TAIL = K - BODY
-SCALAR_SHARE = 2
-T_BANKS = 6
-LOAD_AHEAD = 8
-STATS_AHEAD = 6
-NORM_AHEAD = 4
+SCALAR_SHARE = 1
+LOAD_AHEAD = 6
+STATS_AHEAD = 4
+NORM_AHEAD = 2
 
 FLOPS = 2 * KINDS * ROWS * K * D_OUT
 
@@ -66,7 +65,7 @@ def tile_featureprojector_pa_t_kernel(
         u_pool = ctx.enter_context(tc.tile_pool(name="u_pool", bufs=NORM_AHEAD + 2))
         q_pool = ctx.enter_context(tc.tile_pool(name="q_pool", bufs=3))
         o_pool = ctx.enter_context(tc.tile_pool(name="o_pool", bufs=3))
-        psum_t = ctx.enter_context(tc.psum_pool(name="psum_t", bufs=T_BANKS))
+        psum_t = ctx.enter_context(tc.psum_pool(name="psum_t", bufs=6))
         psum_o = ctx.enter_context(tc.psum_pool(name="psum_o", bufs=2))
 
         ts_bf = keep.tile([P, KINDS, TILES], BF16, name="ts_bf")
@@ -238,25 +237,22 @@ def tile_featureprojector_pa_t_kernel(
             )
             return u
 
-        def transpose_bank(m):
-            g, j = divmod(m, PACK)
-            tp = psum_t.tile([P, GROUP * P], F32, name="tp")
-            for i in range(GROUP):
-                nc.tensor.transpose(tp[:, i * P : (i + 1) * P], u_tiles[g][:, i, j * P : (j + 1) * P], identity[:])
-            return tp
-
-        def scale_bank(m):
-            g, j = divmod(m, PACK)
+        def transpose_and_scale(g):
             kind = g // GROUPS
-            if j == 0:
-                plane_tiles[g] = q_pool.tile([P, PACK, GROUP * P], BF16, name="planes")
-            nc.scalar.activation(
-                out=plane_tiles[g][:, j, :],
-                in_=banks[m][:],
-                func=ACT.Identity,
-                scale=col[:, 8 * kind + j : 8 * kind + j + 1],
-                bias=col[:, 8 * kind + PACK + j : 8 * kind + PACK + j + 1],
-            )
+            u = u_tiles[g]
+            planes = q_pool.tile([P, PACK, GROUP * P], BF16, name="planes")
+            for j in range(PACK):
+                tp = psum_t.tile([P, GROUP * P], F32, name="tp")
+                for i in range(GROUP):
+                    nc.tensor.transpose(tp[:, i * P : (i + 1) * P], u[:, i, j * P : (j + 1) * P], identity[:])
+                nc.scalar.activation(
+                    out=planes[:, j, :],
+                    in_=tp[:],
+                    func=ACT.Identity,
+                    scale=col[:, 8 * kind + j : 8 * kind + j + 1],
+                    bias=col[:, 8 * kind + PACK + j : 8 * kind + PACK + j + 1],
+                )
+            return planes
 
         def regroup(g):
             planes = plane_tiles[g]
@@ -276,10 +272,10 @@ def tile_featureprojector_pa_t_kernel(
             )
             return codes, scales
 
-        def project(g):
-            kind = g // GROUPS
-            codes, scales = code_tiles[g]
-            accs = []
+        def project_and_store(g, codes, scales):
+            kind, first = divmod(g, GROUPS)
+            first *= GROUP
+            o_sb = o_pool.tile([P, GROUP, D_OUT], F32, name="o_sb")
             for pair in range(GROUP // 2):
                 acc = psum_o.tile([P, 2, D_OUT], F32, name="acc")
                 for i in range(2):
@@ -293,43 +289,26 @@ def tile_featureprojector_pa_t_kernel(
                         start=True,
                         stop=True,
                     )
-                accs.append(acc)
-            return accs
-
-        def gelu_and_store(g):
-            kind, first = divmod(g, GROUPS)
-            first *= GROUP
-            o_sb = o_pool.tile([P, GROUP, D_OUT], F32, name="o_sb")
-            for pair in range(GROUP // 2):
-                nc.scalar.activation(out=o_sb[:, 2 * pair : 2 * pair + 2, :], in_=acc_tiles[g][pair][:], func=ACT.Gelu)
+                nc.scalar.activation(out=o_sb[:, 2 * pair : 2 * pair + 2, :], in_=acc[:], func=ACT.Gelu)
             out_rows = out[kind].rearrange("(p t) d -> p t d", t=TILES)
             nc.sync.dma_start(out=out_rows[:, first : first + GROUP, :], in_=o_sb[:])
 
         n_groups = KINDS * GROUPS
         row_stats = {}
         u_tiles = {}
-        banks = {}
         plane_tiles = {}
         grouped_tiles = {}
-        code_tiles = {}
-        acc_tiles = {}
         with tc.manual_schedule():
-            for n in range(-STATS_AHEAD, n_groups + 2):
-                if 0 <= n - 2 < n_groups:
-                    code_tiles[n - 2] = quantise(n - 2)
-                    acc_tiles[n - 2] = project(n - 2)
-                for j in range(PACK):
-                    if 0 <= n < n_groups:
-                        scale_bank(PACK * n + j)
-                    ahead = PACK * n + j + T_BANKS
-                    if 0 <= ahead < PACK * n_groups:
-                        banks[ahead] = transpose_bank(ahead)
-                if 0 <= n - 1 < n_groups:
+            for n in range(-STATS_AHEAD, n_groups + 1):
+                if 0 <= n - 1:
                     grouped_tiles[n - 1] = regroup(n - 1)
-                if 0 <= n - 2 < n_groups:
-                    gelu_and_store(n - 2)
+                if 0 <= n < n_groups:
+                    plane_tiles[n] = transpose_and_scale(n)
                 if 0 <= n + NORM_AHEAD < n_groups:
                     u_tiles[n + NORM_AHEAD] = normalise(n + NORM_AHEAD)
+                if 0 <= n - 1:
+                    codes, scales = quantise(n - 1)
+                    project_and_store(n - 1, codes, scales)
                 if LOAD_AHEAD - STATS_AHEAD <= n + LOAD_AHEAD < n_groups:
                     x_tiles[n + LOAD_AHEAD] = load_group(n + LOAD_AHEAD)
                 if n + STATS_AHEAD < n_groups:

@@ -27,7 +27,8 @@ LN_EPS = 1e-5
 ROUND_MAGIC = 12582912.0
 BODY = 496
 TAIL = K - BODY
-SCALAR_SHARE = 1
+VECTOR_SHARE = 1
+SCALAR_SHARE = 2
 LOAD_AHEAD = 6
 STATS_AHEAD = 4
 NORM_AHEAD = 2
@@ -202,7 +203,16 @@ def tile_featureprojector_pa_t_kernel(
             )
             u = u_pool.tile([P, GROUP, K], F32, name="u")
             for i in range(GROUP):
-                if i < SCALAR_SHARE:
+                if i < VECTOR_SHARE:
+                    nc.vector.tensor_scalar(
+                        out=u[:, i, 0:BODY],
+                        in0=x_sb[:, i, 0:BODY],
+                        scalar1=mean_var[:, i, 0:1],
+                        scalar2=rstd[:, i, :],
+                        op0=ALU.subtract,
+                        op1=ALU.mult,
+                    )
+                elif i < VECTOR_SHARE + SCALAR_SHARE:
                     nc.scalar.activation(
                         out=u[:, i, 0:BODY],
                         in_=x_sb[:, i, 0:BODY],

import math
from contextlib import ExitStack

import concourse.mybir as mybir
from concourse.masks import make_identity

F32 = mybir.dt.float32
BF16 = mybir.dt.bfloat16
U32 = mybir.dt.uint32
U8 = mybir.dt.uint8
FP8X4 = mybir.dt.float8_e4m3fn_x4
ALU = mybir.AluOpType
ACT = mybir.ActivationFunctionType

P = 128
ROWS = 8192
RAW = 500
T2V = 12
K = RAW + T2V
PACK = 4
D_OUT = 256
KINDS = 2
TILES = ROWS // P
GROUP = 4
GROUPS = TILES // GROUP
LN_EPS = 1e-5
ROUND_MAGIC = 12582912.0
BODY = 496
TAIL = K - BODY
VECTOR_SHARE = 1
SCALAR_SHARE = 2
LOAD_AHEAD = 6
STATS_AHEAD = 4
NORM_AHEAD = 2

FLOPS = 2 * KINDS * ROWS * K * D_OUT


def tile_featureprojector_pa_t_kernel(
    tc,
    x_bill,
    ts_bill,
    x_bill_version,
    ts_bill_version,
    w0,
    w,
    b,
    gamma_bill,
    beta_bill,
    W_bill,
    gamma_bill_version,
    beta_bill_version,
    W_bill_version,
    out,
):
    nc = tc.nc
    xs = [x_bill, x_bill_version]
    stamps = [ts_bill, ts_bill_version]
    weights = [W_bill, W_bill_version]
    column_vectors = [gamma_bill, beta_bill, gamma_bill_version, beta_bill_version]

    with ExitStack() as ctx:
        keep = ctx.enter_context(tc.tile_pool(name="keep", bufs=1))
        x_pool = ctx.enter_context(tc.tile_pool(name="x_pool", bufs=LOAD_AHEAD - NORM_AHEAD + 2))
        small = ctx.enter_context(tc.tile_pool(name="small", bufs=STATS_AHEAD - NORM_AHEAD + 2))
        u_pool = ctx.enter_context(tc.tile_pool(name="u_pool", bufs=NORM_AHEAD + 2))
        q_pool = ctx.enter_context(tc.tile_pool(name="q_pool", bufs=3))
        o_pool = ctx.enter_context(tc.tile_pool(name="o_pool", bufs=3))
        psum_t = ctx.enter_context(tc.psum_pool(name="psum_t", bufs=6))
        psum_o = ctx.enter_context(tc.psum_pool(name="psum_o", bufs=2))

        ts_bf = keep.tile([P, KINDS, TILES], BF16, name="ts_bf")
        for kind in range(KINDS):
            nc.sync.dma_start(out=ts_bf[:, kind, :], in_=stamps[kind].rearrange("(p t) -> p t", t=TILES))
        w0_bf = keep.tile([P, 1], BF16, name="w0_bf")
        w_bf = keep.tile([P, T2V - 1], BF16, name="w_bf")
        b_bf = keep.tile([P, T2V], BF16, name="b_bf")
        nc.sync.dma_start(out=w0_bf[:], in_=w0.partition_broadcast(P))
        nc.sync.dma_start(out=w_bf[:], in_=w.partition_broadcast(P))
        nc.sync.dma_start(out=b_bf[:], in_=b.partition_broadcast(P))

        def load_group(g):
            kind, first = divmod(g, GROUPS)
            first *= GROUP
            x_sb = x_pool.tile([P, GROUP, RAW], BF16, name="x_sb")
            rows = xs[kind].rearrange("(p t) k -> p t k", t=TILES)
            nc.sync.dma_start(out=x_sb[:], in_=rows[:, first : first + GROUP, :])
            return x_sb

        x_tiles = {0: load_group(0)}

        vec_bf = keep.tile([P, P], BF16, name="vec_bf")
        nc.vector.memset(vec_bf[:], 0.0)
        for v in range(len(column_vectors)):
            nc.sync.dma_start(
                out=vec_bf[PACK * v : PACK * (v + 1), :],
                in_=column_vectors[v].rearrange("(j c) -> j c", c=P),
            )
        w_raw = []
        for kind in range(KINDS):
            raw = keep.tile([P, PACK, D_OUT], BF16, name="w_raw%d" % kind)
            nc.sync.dma_start(out=raw[:], in_=weights[kind].rearrange("(t p) n -> p t n", p=P))
            w_raw.append(raw)
        for g in range(1, LOAD_AHEAD - STATS_AHEAD):
            x_tiles[g] = load_group(g)

        identity = keep.tile([P, P], F32, name="identity")
        make_identity(nc, identity[:])
        neg_half = keep.tile([P, GROUP, 1], F32, name="neg_half")
        nc.gpsimd.memset(neg_half[:], -0.5)

        slope = keep.tile([P, T2V], F32, name="slope")
        phase = keep.tile([P, T2V], F32, name="phase")
        turn = 1.0 / (2.0 * math.pi)
        nc.vector.tensor_copy(out=slope[:, 0:1], in_=w0_bf[:])
        nc.vector.tensor_copy(out=phase[:, 0:1], in_=b_bf[:, 0:1])
        nc.vector.tensor_scalar(out=slope[:, 1:T2V], in0=w_bf[:], scalar1=turn, scalar2=None, op0=ALU.mult)
        nc.vector.tensor_scalar(out=phase[:, 1:T2V], in0=b_bf[:, 1:T2V], scalar1=turn, scalar2=None, op0=ALU.mult)
        all_tiles = KINDS * TILES
        feat = keep.tile([P, T2V, all_tiles], F32, name="feat")
        for j in range(T2V):
            nc.scalar.activation(
                out=feat[:, j, :],
                in_=ts_bf[:].rearrange("p a t -> p (a t)"),
                func=ACT.Identity,
                scale=slope[:, j : j + 1],
                bias=phase[:, j : j + 1],
            )
        sines = feat[:, 1:T2V, :]
        whole = keep.tile([P, T2V - 1, all_tiles], F32, name="whole")
        nc.vector.tensor_scalar(
            out=whole[:], in0=sines, scalar1=ROUND_MAGIC, scalar2=ROUND_MAGIC, op0=ALU.add, op1=ALU.subtract
        )
        nc.vector.tensor_tensor(out=sines, in0=sines, in1=whole[:], op=ALU.subtract)
        nc.scalar.activation(out=sines, in_=sines, func=ACT.Sin, scale=2.0 * math.pi)

        squares = keep.tile([P, T2V, all_tiles], F32, name="squares")
        nc.scalar.activation(out=squares[:], in_=feat[:], func=ACT.Square)
        feat_sum = keep.tile([P, all_tiles], F32, name="feat_sum")
        feat_sq = keep.tile([P, all_tiles], F32, name="feat_sq")
        nc.vector.tensor_reduce(
            out=feat_sum[:], in_=feat[:].rearrange("p j g -> p g j"), axis=mybir.AxisListType.X, op=ALU.add
        )
        nc.vector.tensor_reduce(
            out=feat_sq[:], in_=squares[:].rearrange("p j g -> p g j"), axis=mybir.AxisListType.X, op=ALU.add
        )
        stats = keep.tile([P, all_tiles, 9], F32, name="stats")
        feat_stats = stats[:, :, 6:9]
        nc.vector.memset(feat_stats[:, :, 0:1], float(T2V))
        nc.vector.tensor_scalar(
            out=feat_stats[:, :, 1:2], in0=feat_sum[:].unsqueeze(2), scalar1=1.0 / T2V, scalar2=None, op0=ALU.mult
        )
        nc.vector.tensor_tensor(
            out=feat_stats[:, :, 2:3], in0=feat_sum[:].unsqueeze(2), in1=feat_stats[:, :, 1:2], op=ALU.mult
        )
        nc.vector.tensor_tensor(
            out=feat_stats[:, :, 2:3], in0=feat_sq[:].unsqueeze(2), in1=feat_stats[:, :, 2:3], op=ALU.subtract
        )
        nc.vector.tensor_scalar(
            out=feat_stats[:, :, 2:3], in0=feat_stats[:, :, 2:3], scalar1=K * LN_EPS, scalar2=None, op0=ALU.add
        )

        vec_f32 = keep.tile([P, P], F32, name="vec_f32")
        nc.vector.tensor_copy(out=vec_f32[:], in_=vec_bf[:])
        vec_t = psum_t.tile([P, PACK * P], F32, name="tp")
        nc.tensor.transpose(vec_t[:, 0:P], vec_f32[:], identity[:])
        col = keep.tile([P, PACK * len(column_vectors)], F32, name="col")
        nc.vector.tensor_copy(out=col[:], in_=vec_t[:, 0 : PACK * len(column_vectors)])

        w_codes = []
        w_scales = []
        for kind in range(KINDS):
            grouped_w = keep.tile([P, D_OUT, PACK], BF16, name="grouped_w%d" % kind, align_bytes=64)
            nc.scalar.copy(
                out=grouped_w[:].rearrange("p (c i) t -> p c t i", i=4),
                in_=w_raw[kind][:].rearrange("p t (c i) -> p c t i", i=4),
            )
            codes = keep.tile([P, D_OUT], U32, name="w_codes%d" % kind, align_bytes=64)
            scales = keep.tile([P, D_OUT], U8, name="w_scales%d" % kind, align_bytes=64)
            nc.vector.quantize_mx(
                out=codes[:].bitcast(FP8X4), scales=scales[:], in_=grouped_w[:].rearrange("p n t -> p (n t)")
            )
            w_codes.append(codes)
            w_scales.append(scales)

        def statistics(g):
            x_sb = x_tiles[g]
            mean_var = small.tile([P, GROUP, 2], F32, name="mean_var")
            for i in range(GROUP):
                nc.vector.bn_stats(out=stats[:, g * GROUP + i, 0:6], in_=x_sb[:, i, :])
            for i in range(GROUP):
                nc.vector.bn_aggr(out=mean_var[:, i, :], in_=stats[:, g * GROUP + i, :])
            rstd = small.tile([P, GROUP, 1], F32, name="rstd")
            nc.gpsimd.tensor_tensor(out=rstd[:], in0=mean_var[:, :, 1:2], in1=neg_half[:], op=ALU.pow)
            return mean_var, rstd

        def normalise(g):
            x_sb = x_tiles[g]
            mean_var, rstd = row_stats[g]
            shift = small.tile([P, GROUP, 1], F32, name="shift")
            nc.vector.scalar_tensor_tensor(
                out=shift[:], in0=mean_var[:, :, 0:1], scalar=-1.0, in1=rstd[:], op0=ALU.mult, op1=ALU.mult
            )
            u = u_pool.tile([P, GROUP, K], F32, name="u")
            for i in range(GROUP):
                if i < VECTOR_SHARE:
                    nc.vector.tensor_scalar(
                        out=u[:, i, 0:BODY],
                        in0=x_sb[:, i, 0:BODY],
                        scalar1=mean_var[:, i, 0:1],
                        scalar2=rstd[:, i, :],
                        op0=ALU.subtract,
                        op1=ALU.mult,
                    )
                elif i < VECTOR_SHARE + SCALAR_SHARE:
                    nc.scalar.activation(
                        out=u[:, i, 0:BODY],
                        in_=x_sb[:, i, 0:BODY],
                        func=ACT.Identity,
                        scale=rstd[:, i, :],
                        bias=shift[:, i, :],
                    )
                else:
                    nc.gpsimd.tensor_scalar(
                        out=u[:, i, 0:BODY],
                        in0=x_sb[:, i, 0:BODY],
                        scalar1=rstd[:, i, :],
                        scalar2=shift[:, i, :],
                        op0=ALU.mult,
                        op1=ALU.add,
                    )
            centred = small.tile([P, GROUP, TAIL], F32, name="centred")
            nc.gpsimd.tensor_tensor(
                out=centred[:, :, 0 : RAW - BODY],
                in0=x_sb[:, :, BODY:RAW],
                in1=mean_var[:, :, 0:1].to_broadcast([P, GROUP, RAW - BODY]),
                op=ALU.subtract,
            )
            nc.gpsimd.tensor_tensor(
                out=centred[:, :, RAW - BODY : TAIL],
                in0=feat[:, :, g * GROUP : (g + 1) * GROUP].rearrange("p j g -> p g j"),
                in1=mean_var[:, :, 0:1].to_broadcast([P, GROUP, T2V]),
                op=ALU.subtract,
            )
            nc.gpsimd.tensor_tensor(
                out=u[:, :, BODY:K], in0=centred[:], in1=rstd[:].to_broadcast([P, GROUP, TAIL]), op=ALU.mult
            )
            return u

        def transpose_and_scale(g):
            kind = g // GROUPS
            u = u_tiles[g]
            planes = q_pool.tile([P, PACK, GROUP * P], BF16, name="planes")
            for j in range(PACK):
                tp = psum_t.tile([P, GROUP * P], F32, name="tp")
                for i in range(GROUP):
                    nc.tensor.transpose(tp[:, i * P : (i + 1) * P], u[:, i, j * P : (j + 1) * P], identity[:])
                nc.scalar.activation(
                    out=planes[:, j, :],
                    in_=tp[:],
                    func=ACT.Identity,
                    scale=col[:, 8 * kind + j : 8 * kind + j + 1],
                    bias=col[:, 8 * kind + PACK + j : 8 * kind + PACK + j + 1],
                )
            return planes

        def regroup(g):
            planes = plane_tiles[g]
            grouped = q_pool.tile([P, GROUP * P, PACK], BF16, name="grouped", align_bytes=64)
            nc.vector.tensor_copy(
                out=grouped[:].rearrange("p (c i) t -> p c t i", i=4),
                in_=planes[:].rearrange("p t (c i) -> p c t i", i=4),
            )
            return grouped

        def quantise(g):
            grouped = grouped_tiles[g]
            codes = q_pool.tile([P, GROUP * P], U32, name="codes", align_bytes=64)
            scales = q_pool.tile([P, GROUP * P], U8, name="scales", align_bytes=64)
            nc.vector.quantize_mx(
                out=codes[:].bitcast(FP8X4), scales=scales[:], in_=grouped[:].rearrange("p r t -> p (r t)")
            )
            return codes, scales

        def project_and_store(g, codes, scales):
            kind, first = divmod(g, GROUPS)
            first *= GROUP
            o_sb = o_pool.tile([P, GROUP, D_OUT], F32, name="o_sb")
            for pair in range(GROUP // 2):
                acc = psum_o.tile([P, 2, D_OUT], F32, name="acc")
                for i in range(2):
                    rows = slice((2 * pair + i) * P, (2 * pair + i + 1) * P)
                    nc.tensor.matmul_mx(
                        out=acc[:, i, :],
                        lhsT=codes[:, rows].bitcast(FP8X4),
                        lhsT_scale=scales[:, rows],
                        rhs=w_codes[kind][:].bitcast(FP8X4),
                        rhs_scale=w_scales[kind][:],
                        start=True,
                        stop=True,
                    )
                nc.scalar.activation(out=o_sb[:, 2 * pair : 2 * pair + 2, :], in_=acc[:], func=ACT.Gelu)
            out_rows = out[kind].rearrange("(p t) d -> p t d", t=TILES)
            nc.sync.dma_start(out=out_rows[:, first : first + GROUP, :], in_=o_sb[:])

        n_groups = KINDS * GROUPS
        row_stats = {}
        u_tiles = {}
        plane_tiles = {}
        grouped_tiles = {}
        with tc.manual_schedule():
            for n in range(-STATS_AHEAD, n_groups + 1):
                if 0 <= n - 1:
                    grouped_tiles[n - 1] = regroup(n - 1)
                if 0 <= n < n_groups:
                    plane_tiles[n] = transpose_and_scale(n)
                if 0 <= n + NORM_AHEAD < n_groups:
                    u_tiles[n + NORM_AHEAD] = normalise(n + NORM_AHEAD)
                if 0 <= n - 1:
                    codes, scales = quantise(n - 1)
                    project_and_store(n - 1, codes, scales)
                if LOAD_AHEAD - STATS_AHEAD <= n + LOAD_AHEAD < n_groups:
                    x_tiles[n + LOAD_AHEAD] = load_group(n + LOAD_AHEAD)
                if n + STATS_AHEAD < n_groups:
                    row_stats[n + STATS_AHEAD] = statistics(n + STATS_AHEAD)
